import numpy as np
import ml_dtypes


def mxq(x, axis, fmt="e4m3"):
    dtype, down = {"e4m3": (ml_dtypes.float8_e4m3fn, 7), "e5m2": (ml_dtypes.float8_e5m2, 14)}[fmt]
    v = np.moveaxis(np.asarray(x, np.float32).astype(ml_dtypes.bfloat16).astype(np.float64), axis, -1)
    blocks = v.reshape(v.shape[:-1] + (-1, 32))
    amax = np.abs(blocks).max(-1, keepdims=True)
    byte = np.maximum(np.where(amax > 0, np.frexp(amax)[1] - 1 + 127, 0) - down, 1)
    scale = np.exp2(byte - 127.0)
    codes = (blocks / scale).astype(np.float32).astype(dtype).astype(np.float64)
    return np.moveaxis((codes * scale).reshape(v.shape), -1, axis)


WIDE = False


def mx_kscale(k):
    if not WIDE:
        return np.ones(k)
    levels = np.array([10, -10, 5, -5, 0])
    if k % 512:
        return np.exp2(np.random.permutation(np.resize(levels, k // 32))).repeat(32)
    a = np.empty((k // 512, 16))
    for p in range(k // 512):
        a[p, :8] = np.random.permutation(np.resize(levels, 8))
        for g in range(8):
            far = levels[np.abs(levels - a[p, g]) >= 10]
            a[p, g + 8] = far[np.random.randint(len(far))]
    return np.exp2(a.ravel()).repeat(32)


BF16 = ml_dtypes.bfloat16


def bf(x):
    return np.asarray(x, np.float32).astype(BF16)


def f64(x):
    return np.asarray(x).astype(np.float64)


E2M1 = np.array([0.0, 0.5, 1.0, 1.5, 2.0, 3.0, 4.0, 6.0, -0.0, -0.5, -1.0, -1.5, -2.0, -3.0, -4.0, -6.0])


def pack_weight(w, fmt):
    k, n = w.shape
    w = f64(bf(w)).reshape(k // 32, 32, n)
    amax = np.abs(w).max(1)
    if fmt == "e4m3":
        byte = np.frexp(amax)[1] - 1 + 127 - 7
    else:
        mant, ex = np.frexp(amax / 6.0)
        byte = np.where(mant > 0.5, ex, ex - 1) + 127
    byte = np.clip(np.where(amax > 0, byte, 1), 1, 254)
    scaled = (w * np.exp2(127.0 - byte)[:, None, :]).reshape(k, n).astype(np.float32)
    by_word = np.ascontiguousarray(scaled.reshape(k // 512, 128, 4, n).transpose(0, 1, 3, 2))
    if fmt == "e4m3":
        words = by_word.astype(ml_dtypes.float8_e4m3fn).view(np.uint8)
    else:
        c = by_word.astype(ml_dtypes.float4_e2m1fn).view(np.uint8) & 0xF
        words = c[..., 0::2] | (c[..., 1::2] << 4)
    return np.ascontiguousarray(words), np.ascontiguousarray(byte.astype(np.uint8).reshape(k // 512, 16, n))


def unpack_weight(words, scales, fmt):
    g, p, n, _ = words.shape
    if fmt == "e4m3":
        vals = np.ascontiguousarray(words).view(ml_dtypes.float8_e4m3fn).astype(np.float64)
    else:
        nib = np.empty((g, p, n, 4), np.uint8)
        nib[..., 0::2] = words & 0xF
        nib[..., 1::2] = words >> 4
        vals = E2M1[nib]
    vals = vals * np.repeat(np.exp2(scales.astype(np.float64) - 127.0), 8, axis=1)[..., None]
    return vals.transpose(0, 1, 3, 2).reshape(g * 512, n)
def pack4(w):
    words, scales = pack_weight(w, "e2m1")
    return words.reshape(words.shape[0], 128, -1), scales


def unpack4(words, scales):
    return unpack_weight(words.reshape(words.shape[0], 128, -1, 2), scales, "e2m1")


B, C, MID, HH, WW = 1, 2048, 512, 32, 32
N = HH * WW


def draw0():
    s, t = mx_kscale(N), mx_kscale(MID)
    a = np.exp(1.5 * np.random.standard_normal((B, N, N)))
    a = a / a.sum(-1, keepdims=True)
    h_x = bf(np.random.standard_normal((B, MID, N)) * 2.0 * t[:, None] / s)
    v_w = np.random.standard_normal((C, MID)) * 3.0 / np.sqrt(MID) / t
    words, scales = pack4(v_w.T)
    return {
        "attn": bf(a * s),
        "h_x": h_x,
        "v_w_words": words,
        "v_w_scales": scales,
        "v_b": bf(np.random.standard_normal(C) * 0.3),
        "x": bf(np.random.standard_normal((B, C, HH, WW))),
    }


def core(attn, h_x, v_w_words, v_w_scales, v_b, x):
    z = mxq(f64(h_x), 2, "e4m3") @ mxq(f64(attn), 2, "e4m3").transpose(0, 2, 1)
    y = (unpack4(v_w_words, v_w_scales).T @ mxq(z, 1, "e4m3")) + f64(v_b)[None, :, None]
    return y.reshape(B, C, HH, WW) + f64(x)


def e4m3fn_bytes(y):
    return np.clip(np.asarray(y, np.float64), -448.0, 448.0).astype(np.float32).astype(ml_dtypes.float8_e4m3fn).view(np.uint8)


def e4m3fn_values(b):
    return np.asarray(b, np.uint8).view(ml_dtypes.float8_e4m3fn).astype(np.float64)


def setup_inputs():
    d = draw0()
    x0 = np.asarray(d['attn']).astype(np.float64)
    s = (np.max(np.abs(x0), axis=(0, 1), keepdims=True) / 448.0).astype(np.float32)
    out = {}
    for k, v in d.items():
        if k == 'attn':
            out['attn_bytes'] = e4m3fn_bytes(x0 / s.astype(np.float64))
            out['attn_scale'] = s
        else:
            out[k] = v
    return out


def reference(attn_bytes, attn_scale, h_x, v_w_words, v_w_scales, v_b, x):
    return core(e4m3fn_values(attn_bytes) * attn_scale.astype(np.float64), h_x, v_w_words, v_w_scales, v_b, x)

@@ -1,0 +1,270 @@
+from contextlib import ExitStack
+
+import concourse.mybir as mybir
+from concourse.masks import make_identity
+
+F32 = mybir.dt.float32
+BF16 = mybir.dt.bfloat16
+I32 = mybir.dt.int32
+U32 = mybir.dt.uint32
+U8 = mybir.dt.uint8
+F8 = mybir.dt.float8_e4m3fn
+FP8X4 = mybir.dt.float8_e4m3fn_x4
+FP4X4 = mybir.dt.float4_e2m1fn_x4
+MULT = mybir.AluOpType.mult
+ADD = mybir.AluOpType.add
+ACT = mybir.ActivationFunctionType
+
+P = 128
+PACK = 4
+K_PASS = P * PACK
+C, MID, N = 2048, 512, 1024
+GROUPS = N // K_PASS
+QUARTERS = 4
+QN = N // QUARTERS
+HN = N // 2
+O_TILES = C // P
+X_TILES = 4
+FLOPS = 2 * MID * N * N + 2 * C * MID * N
+
+SHARED = ((0, 2, 6, 8, 14), (5, 9))
+STORE_LAG = 2
+
+
+def tile_soablock_pb_w4_kernel(tc, attn_bytes, attn_scale, h_x, v_w_words, v_w_scales, v_b, x, out):
+    nc = tc.nc
+    with ExitStack() as ctx:
+        keep = ctx.enter_context(tc.tile_pool(name="keep", bufs=1))
+        temp = ctx.enter_context(tc.tile_pool(name="temp", bufs=4))
+        psum = ctx.enter_context(tc.psum_pool(name="psum", bufs=8))
+        ctx.enter_context(tc.manual_schedule())
+
+        def keep_tile(name, shape, dtype):
+            return keep.tile(shape, dtype, name=name, tag=name, align_bytes=64)
+
+        def bank_tile():
+            return psum.tile([P, HN], F32, name="bank", tag="bank")
+
+        scale_kp = keep_tile("scale_kp", [P, GROUPS * PACK], F32)
+        scale_row = keep_tile("scale_row", [P, N], F32)
+        codes_in = [keep_tile(f"codes_in{q}", [P, 2, N], U8) for q in range(QUARTERS)]
+        attn_rows = [keep_tile(f"attn_rows{q}", [P, 2, N], BF16) for q in range(QUARTERS)]
+        hx_rows = [keep_tile(f"hx_rows{i}", [P, 2, N], BF16) for i in range(2)]
+        words = keep_tile("words", [P, 2 * C], U8)
+        word_scales = keep_tile("word_scales", [P, C], U8)
+        bias_rows = keep_tile("bias_rows", [P, P], BF16)
+        bias_cols = keep_tile("bias_cols", [P, O_TILES], F32)
+        xs = [keep_tile(f"xs{i}", [P, X_TILES, N], BF16) for i in range(O_TILES // X_TILES)]
+        attn_kp = [keep_tile(f"attn_kp{q}", [P, GROUPS, QN, PACK], BF16) for q in range(QUARTERS)]
+        attn_codes = [keep_tile(f"attn_codes{q}", [P, GROUPS * QN], U32) for q in range(QUARTERS)]
+        attn_scales = [keep_tile(f"attn_scales{q}", [P, GROUPS * QN], U8) for q in range(QUARTERS)]
+        hx_kp = [keep_tile(f"hx_kp{g}", [P, MID, PACK], BF16) for g in range(GROUPS)]
+        hx_codes = [keep_tile(f"hx_codes{g}", [P, MID], U32) for g in range(GROUPS)]
+        hx_scales = [keep_tile(f"hx_scales{g}", [P, MID], U8) for g in range(GROUPS)]
+        z_kp = [keep_tile(f"z_kp{q}", [P, QN, PACK], BF16) for q in range(QUARTERS)]
+        z_codes = [keep_tile(f"z_codes{h}", [P, HN], U32) for h in range(2)]
+        z_scales = [keep_tile(f"z_scales{h}", [P, HN], U8) for h in range(2)]
+        results = [[keep_tile(f"result{a}_{h}", [P, HN], F32) for h in range(2)] for a in range(O_TILES)]
+        ident = keep_tile("ident", [P, P], F32)
+        ident_bf = keep_tile("ident_bf", [P, P], BF16)
+        dummy = keep_tile("dummy", [P, 1], F32)
+
+        nc.vector.memset(dummy[:], 0.0)
+        nc.vector.memset(bias_rows[:], 0.0)
+        nc.vector.memset(word_scales[:].bitcast(I32), 0)
+        make_identity(nc, ident[:])
+        make_identity(nc, ident_bf[:])
+        nc.scalar.activation(dummy[:], dummy[:], ACT.Identity)
+
+        def load_attn(q):
+            nc.sync.dma_start(out=codes_in[q][:], in_=attn_bytes[0, QN * q : QN * (q + 1), :].rearrange("(r j) m -> r j m", j=2))
+
+        nc.sync.dma_start(
+            out=scale_kp[:].rearrange("p (g t) -> p g t", t=PACK),
+            in_=attn_scale.rearrange("a b (g p t) -> p (a b g) t", g=GROUPS, t=PACK),
+        )
+        load_attn(0)
+        load_attn(1)
+        for i in range(2):
+            nc.sync.dma_start(out=hx_rows[i][:], in_=h_x[0].rearrange("(r t) m -> r t m", t=PACK)[:, 2 * i : 2 * i + 2, :])
+        nc.sync.dma_start(out=bias_rows[0:O_TILES, :], in_=v_b.rearrange("(a p) -> a p", p=P))
+        load_attn(2)
+        load_attn(3)
+        nc.sync.dma_start(out=words[:], in_=v_w_words[0])
+        for s in range(4):
+            nc.sync.dma_start(out=word_scales[32 * s : 32 * s + 4, :].bitcast(I32), in_=v_w_scales[0, 4 * s : 4 * s + 4, :].bitcast(I32))
+        x_view = x.rearrange("b (a p) h w -> p a (b h w)", p=P)
+        for i in range(O_TILES // X_TILES):
+            nc.sync.dma_start(out=xs[i][:], in_=x_view[:, X_TILES * i : X_TILES * (i + 1), :])
+
+        def busy(count):
+            bank = bank_tile()
+            for i in range(count):
+                nc.tensor.matmul(bank[:, 0:P], lhsT=ident[:], rhs=ident[:], start=True, stop=True)
+
+        def spread(g):
+            bank = bank_tile()
+            for t in range(PACK):
+                column = scale_kp[:, PACK * g + t : PACK * g + t + 1]
+                nc.tensor.transpose(bank[:, P * t : P * (t + 1)], column.to_broadcast([P, P]), ident[:])
+            row = scale_row[:, K_PASS * g : K_PASS * (g + 1)].rearrange("p (k t) -> p k t", t=PACK)
+            nc.scalar.copy(row, bank[:].rearrange("p (t k) -> p k t", t=PACK))
+
+        def product(q, j, first=0, last=N):
+            nc.vector.tensor_tensor(
+                out=attn_rows[q][:, j, first:last],
+                in0=codes_in[q][:, j, first:last].bitcast(F8),
+                in1=scale_row[:, first:last],
+                op=MULT,
+            )
+
+        def turn(rows, g):
+            bank = bank_tile()
+            for j in range(2):
+                row_words = rows[:, j, :].bitcast(F32)
+                for u in range(2):
+                    s = 2 * j + u
+                    nc.tensor.transpose(bank[:, P * s : P * (s + 1)], row_words[:, 256 * g + u : 256 * (g + 1) : 2], ident[:])
+            return bank
+
+        def attn_turn(q, g):
+            bank = turn(attn_rows[q], g)
+            target = attn_kp[q][:, g, :, :].rearrange("p n t -> p (n t)").bitcast(F32)
+            nc.scalar.copy(target.rearrange("p (r s) -> p r s", s=4), bank[:].rearrange("p (s r) -> p r s", s=4))
+
+        def hx_turn(i, g):
+            bank = turn(hx_rows[i], g)
+            target = hx_kp[g][:, 2 * P * i : 2 * P * (i + 1), :].rearrange("p c t -> p (c t)").bitcast(F32)
+            nc.scalar.copy(target.rearrange("p (j r u) -> p j r u", j=2, u=2), bank[:].rearrange("p (j u r) -> p j r u", j=2, u=2))
+
+        def bias_turn():
+            bank = psum.tile([P, P], BF16, name="bank", tag="bank")
+            nc.tensor.transpose(bank[:], bias_rows[:], ident_bf[:])
+            nc.scalar.copy(bias_cols[:], bank[:, 0:O_TILES])
+
+        def quant_attn(q):
+            nc.vector.quantize_mx(out=attn_codes[q][:].bitcast(FP8X4), scales=attn_scales[q][:], in_=attn_kp[q][:].rearrange("p g n t -> p (g n t)"))
+
+        def quant_hx(g):
+            nc.vector.quantize_mx(out=hx_codes[g][:].bitcast(FP8X4), scales=hx_scales[g][:], in_=hx_kp[g][:].rearrange("p c t -> p (c t)"))
+
+        def z_quarter(q):
+            for part in range(QN // P):
+                bank = bank_tile()
+                for t in range(PACK):
+                    for g in range(GROUPS):
+                        cols = slice(QN * g + P * part, QN * g + P * (part + 1))
+                        nc.tensor.matmul_mx(
+                            out=bank[:, P * t : P * (t + 1)],
+                            lhsT=hx_codes[g][:, P * t : P * (t + 1)].bitcast(FP8X4),
+                            lhsT_scale=hx_scales[g][:, P * t : P * (t + 1)],
+                            rhs=attn_codes[q][:, cols].bitcast(FP8X4),
+                            rhs_scale=attn_scales[q][:, cols],
+                            start=(g == 0),
+                            stop=(g == GROUPS - 1),
+                        )
+                nc.scalar.copy(z_kp[q][:, P * part : P * (part + 1), :], bank[:].rearrange("p (t n) -> p n t", t=PACK))
+
+        def quant_z(q):
+            h, cols = q // 2, slice(QN * (q % 2), QN * (q % 2 + 1))
+            nc.vector.quantize_mx(out=z_codes[h][:, cols].bitcast(FP8X4), scales=z_scales[h][:, cols], in_=z_kp[q][:].rearrange("p n t -> p (n t)"))
+
+        y_banks = {}
+        issued = [0, 0]
+
+        def issue_y(h, upto):
+            for a in range(issued[h], min(upto, O_TILES)):
+                y_banks[a, h] = bank_tile()
+                nc.tensor.matmul_mx(
+                    out=y_banks[a, h][:],
+                    lhsT=words[:, 2 * P * a : 2 * P * (a + 1)].bitcast(FP4X4),
+                    lhsT_scale=word_scales[:, P * a : P * (a + 1)],
+                    rhs=z_codes[h][:].bitcast(FP8X4),
+                    rhs_scale=z_scales[h][:],
+                    start=True,
+                    stop=True,
+                )
+                issued[h] = a + 1
+
+        out_view = out.rearrange("b (a p) h w -> a p (b h w)", p=P)
+
+        def store(a, h):
+            nc.sync.dma_start(out=out_view[a][:, HN * h : HN * (h + 1)], in_=results[a][h][:])
+
+        waiting = []
+
+        def finish_y(a, h):
+            bias = bias_cols[:, a : a + 1]
+            residual = xs[a // X_TILES][:, a % X_TILES, HN * h : HN * (h + 1)]
+            if a in SHARED[h]:
+                partial = temp.tile([P, HN], F32, name="partial", tag="partial")
+                nc.scalar.activation(partial[:], y_banks[a, h][:], ACT.Identity, bias=bias)
+                nc.gpsimd.tensor_tensor(out=results[a][h][:], in0=partial[:], in1=residual, op=ADD)
+                waiting.append([a, h, STORE_LAG])
+            else:
+                nc.vector.scalar_tensor_tensor(out=results[a][h][:], in0=y_banks[a, h][:], scalar=bias, in1=residual, op0=ADD, op1=ADD)
+                store(a, h)
+                for entry in list(waiting):
+                    entry[2] -= 1
+                    if entry[2] == 0:
+                        store(entry[0], entry[1])
+                        waiting.remove(entry)
+
+        busy(3)
+        for g in range(GROUPS):
+            spread(g)
+            busy(1)
+        for g in range(GROUPS):
+            for j in range(2):
+                product(0, j, K_PASS * g, K_PASS * (g + 1))
+        for j in range(2):
+            product(1, j)
+        for i in range(2):
+            for g in range(GROUPS):
+                hx_turn(i, g)
+                busy(1)
+        attn_turn(0, 0)
+        bias_turn()
+        for q, g in ((0, 1), (1, 0), (1, 1)):
+            busy(1)
+            attn_turn(q, g)
+        for g in range(GROUPS):
+            quant_hx(g)
+        quant_attn(0)
+        z_quarter(0)
+        product(2, 0)
+        quant_attn(1)
+        z_quarter(1)
+        product(2, 1)
+        product(3, 0)
+        for g in range(GROUPS):
+            busy(1)
+            attn_turn(2, g)
+        quant_z(0)
+        quant_z(1)
+        issue_y(0, 5)
+        product(3, 1)
+
+        for a in range(O_TILES):
+            if a == 3:
+                for g in range(GROUPS):
+                    attn_turn(3, g)
+            elif a == 4:
+                quant_attn(2)
+            elif a == 6:
+                quant_attn(3)
+            elif a == 9:
+                z_quarter(2)
+            elif a == 12:
+                z_quarter(3)
+            elif a == 13:
+                quant_z(2)
+            elif a == 15:
+                quant_z(3)
+            if a >= 3:
+                issue_y(0, a + 4)
+            finish_y(a, 0)
+
+        for a in range(O_TILES):
+            issue_y(1, a + 6)
+            finish_y(a, 1)

@@ -28,7 +28,10 @@ X_TILES = 4
 FLOPS = 2 * MID * N * N + 2 * C * MID * N
 
 SHARED = ((0, 2, 6, 8, 14), (5, 9))
-STORE_LAG = 2
+STORES = (
+    ((1, 1, 1), (3, 1, 3), (0, 1, 3), (4, 1, 4), (2, 1, 4), (5, 1, 5), (7, 1, 7), (9, 1, 9), (6, 1, 9), (10, 1, 10), (8, 1, 10), (11, 1, 11), (12, 1, 12), (13, 1, 13), (14, 2, 15)),
+    ((0, 2, 1), (2, 2, 3), (4, 4, 7), (8, 4, 11), (12, 4, 15)),
+)
 
 
 def tile_soablock_pb_w4_kernel(tc, attn_bytes, attn_scale, h_x, v_w_words, v_w_scales, v_b, x, out):
@@ -64,7 +67,7 @@ def tile_soablock_pb_w4_kernel(tc, attn_bytes, attn_scale, h_x, v_w_words, v_w_s
         z_kp = [keep_tile(f"z_kp{q}", [P, QN, PACK], BF16) for q in range(QUARTERS)]
         z_codes = [keep_tile(f"z_codes{h}", [P, HN], U32) for h in range(2)]
         z_scales = [keep_tile(f"z_scales{h}", [P, HN], U8) for h in range(2)]
-        results = [[keep_tile(f"result{a}_{h}", [P, HN], F32) for h in range(2)] for a in range(O_TILES)]
+        results = [keep_tile(f"result{i}", [P, X_TILES, N], F32) for i in range(O_TILES // X_TILES)]
         ident = keep_tile("ident", [P, P], F32)
         ident_bf = keep_tile("ident_bf", [P, P], BF16)
         dummy = keep_tile("dummy", [P, 1], F32)
@@ -84,15 +87,15 @@ def tile_soablock_pb_w4_kernel(tc, attn_bytes, attn_scale, h_x, v_w_words, v_w_s
             in_=attn_scale.rearrange("a b (g p t) -> p (a b g) t", g=GROUPS, t=PACK),
         )
         load_attn(0)
-        load_attn(1)
         for i in range(2):
             nc.sync.dma_start(out=hx_rows[i][:], in_=h_x[0].rearrange("(r t) m -> r t m", t=PACK)[:, 2 * i : 2 * i + 2, :])
+        load_attn(1)
         nc.sync.dma_start(out=bias_rows[0:O_TILES, :], in_=v_b.rearrange("(a p) -> a p", p=P))
         load_attn(2)
         load_attn(3)
         nc.sync.dma_start(out=words[:], in_=v_w_words[0])
-        for s in range(4):
-            nc.sync.dma_start(out=word_scales[32 * s : 32 * s + 4, :].bitcast(I32), in_=v_w_scales[0, 4 * s : 4 * s + 4, :].bitcast(I32))
+        for r in range(4):
+            nc.sync.dma_start(out=word_scales[r:P:32, :].bitcast(I32), in_=v_w_scales[0, r:16:4, :].bitcast(I32))
         x_view = x.rearrange("b (a p) h w -> p a (b h w)", p=P)
         for i in range(O_TILES // X_TILES):
             nc.sync.dma_start(out=xs[i][:], in_=x_view[:, X_TILES * i : X_TILES * (i + 1), :])
@@ -170,45 +173,52 @@ def tile_soablock_pb_w4_kernel(tc, attn_bytes, attn_scale, h_x, v_w_words, v_w_s
             nc.vector.quantize_mx(out=z_codes[h][:, cols].bitcast(FP8X4), scales=z_scales[h][:, cols], in_=z_kp[q][:].rearrange("p n t -> p (n t)"))
 
         y_banks = {}
+
+        def y_matmul(a, h):
+            y_banks[a, h] = bank_tile()
+            nc.tensor.matmul_mx(
+                out=y_banks[a, h][:],
+                lhsT=words[:, 2 * P * a : 2 * P * (a + 1)].bitcast(FP4X4),
+                lhsT_scale=word_scales[:, P * a : P * (a + 1)],
+                rhs=z_codes[h][:].bitcast(FP8X4),
+                rhs_scale=z_scales[h][:],
+                start=True,
+                stop=True,
+            )
+
+        def finish_y(a, h, shared=False):
+            bias = bias_cols[:, a : a + 1]
+            cols = slice(HN * h, HN * (h + 1))
+            residual = xs[a // X_TILES][:, a % X_TILES, cols]
+            result = results[a // X_TILES][:, a % X_TILES, cols]
+            if shared:
+                partial = temp.tile([P, HN], F32, name="partial", tag="partial")
+                nc.scalar.activation(partial[:], y_banks[a, h][:], ACT.Identity, bias=bias)
+                nc.gpsimd.tensor_tensor(out=result, in0=partial[:], in1=residual, op=ADD)
+            else:
+                nc.vector.scalar_tensor_tensor(out=result, in0=y_banks[a, h][:], scalar=bias, in1=residual, op0=ADD, op1=ADD)
+
+        out_view = out.rearrange("b (a p) h w -> p a (b h w)", p=P)
+
+        def store(a, count, first=0, last=N):
+            i = a % X_TILES
+            nc.sync.dma_start(out=out_view[:, a : a + count, first:last], in_=results[a // X_TILES][:, i : i + count, first:last])
+
         issued = [0, 0]
+
 
         def issue_y(h, upto):
             for a in range(issued[h], min(upto, O_TILES)):
-                y_banks[a, h] = bank_tile()
-                nc.tensor.matmul_mx(
-                    out=y_banks[a, h][:],
-                    lhsT=words[:, 2 * P * a : 2 * P * (a + 1)].bitcast(FP4X4),
-                    lhsT_scale=word_scales[:, P * a : P * (a + 1)],
-                    rhs=z_codes[h][:].bitcast(FP8X4),
-                    rhs_scale=z_scales[h][:],
-                    start=True,
-                    stop=True,
-                )
+                y_matmul(a, h)
                 issued[h] = a + 1
 
-        out_view = out.rearrange("b (a p) h w -> a p (b h w)", p=P)
 
-        def store(a, h):
-            nc.sync.dma_start(out=out_view[a][:, HN * h : HN * (h + 1)], in_=results[a][h][:])
+        def finish_and_store(a, h):
+            finish_y(a, h, a in SHARED[h])
+            for first, count, after in STORES[h]:
+                if after == a:
+                    store(first, count, HN * h, HN * (h + 1))
 
-        waiting = []
-
-        def finish_y(a, h):
-            bias = bias_cols[:, a : a + 1]
-            residual = xs[a // X_TILES][:, a % X_TILES, HN * h : HN * (h + 1)]
-            if a in SHARED[h]:
-                partial = temp.tile([P, HN], F32, name="partial", tag="partial")
-                nc.scalar.activation(partial[:], y_banks[a, h][:], ACT.Identity, bias=bias)
-                nc.gpsimd.tensor_tensor(out=results[a][h][:], in0=partial[:], in1=residual, op=ADD)
-                waiting.append([a, h, STORE_LAG])
-            else:
-                nc.vector.scalar_tensor_tensor(out=results[a][h][:], in0=y_banks[a, h][:], scalar=bias, in1=residual, op0=ADD, op1=ADD)
-                store(a, h)
-                for entry in list(waiting):
-                    entry[2] -= 1
-                    if entry[2] == 0:
-                        store(entry[0], entry[1])
-                        waiting.remove(entry)
 
         busy(3)
         for g in range(GROUPS):
@@ -263,8 +273,8 @@ def tile_soablock_pb_w4_kernel(tc, attn_bytes, attn_scale, h_x, v_w_words, v_w_s
                 quant_z(3)
             if a >= 3:
                 issue_y(0, a + 4)
-            finish_y(a, 0)
+            finish_and_store(a, 0)
 
         for a in range(O_TILES):
             issue_y(1, a + 6)
-            finish_y(a, 1)
+            finish_and_store(a, 1)

@@ -24,21 +24,17 @@ QUARTERS = 4
 QN = N // QUARTERS
 HN = N // 2
 O_TILES = C // P
-X_TILES = 4
+X_TILES = 8
 FLOPS = 2 * MID * N * N + 2 * C * MID * N
 
-SHARED = ((0, 2, 6, 8, 14), (5, 9))
-STORES = (
-    ((1, 1, 1), (3, 1, 3), (0, 1, 3), (4, 1, 4), (2, 1, 4), (5, 1, 5), (7, 1, 7), (9, 1, 9), (6, 1, 9), (10, 1, 10), (8, 1, 10), (11, 1, 11), (12, 1, 12), (13, 1, 13), (14, 2, 15)),
-    ((0, 2, 1), (2, 2, 3), (4, 4, 7), (8, 4, 11), (12, 4, 15)),
-)
+SIZES = ((2, 2), (2, 2), (4,), (4,))
 
 
 def tile_soablock_pb_w4_kernel(tc, attn_bytes, attn_scale, h_x, v_w_words, v_w_scales, v_b, x, out):
     nc = tc.nc
     with ExitStack() as ctx:
         keep = ctx.enter_context(tc.tile_pool(name="keep", bufs=1))
-        temp = ctx.enter_context(tc.tile_pool(name="temp", bufs=4))
+        temp = ctx.enter_context(tc.tile_pool(name="temp", bufs=1))
         psum = ctx.enter_context(tc.psum_pool(name="psum", bufs=8))
         ctx.enter_context(tc.manual_schedule())
 
@@ -50,8 +46,8 @@ def tile_soablock_pb_w4_kernel(tc, attn_bytes, attn_scale, h_x, v_w_words, v_w_s
 
         scale_kp = keep_tile("scale_kp", [P, GROUPS * PACK], F32)
         scale_row = keep_tile("scale_row", [P, N], F32)
-        codes_in = [keep_tile(f"codes_in{q}", [P, 2, N], U8) for q in range(QUARTERS)]
-        attn_rows = [keep_tile(f"attn_rows{q}", [P, 2, N], BF16) for q in range(QUARTERS)]
+        codes_in = [keep_tile(f"codes_in{i}", [P, count, 2, N], U8) for i, count in enumerate((1, 1, 2))]
+        attn_rows = [[keep_tile(f"attn_rows{q}_{g}", [P, 2, K_PASS], BF16) for g in range(GROUPS)] for q in range(QUARTERS)]
         hx_rows = [keep_tile(f"hx_rows{i}", [P, 2, N], BF16) for i in range(2)]
         words = keep_tile("words", [P, 2 * C], U8)
         word_scales = keep_tile("word_scales", [P, C], U8)
@@ -67,7 +63,7 @@ def tile_soablock_pb_w4_kernel(tc, attn_bytes, attn_scale, h_x, v_w_words, v_w_s
         z_kp = [keep_tile(f"z_kp{q}", [P, QN, PACK], BF16) for q in range(QUARTERS)]
         z_codes = [keep_tile(f"z_codes{h}", [P, HN], U32) for h in range(2)]
         z_scales = [keep_tile(f"z_scales{h}", [P, HN], U8) for h in range(2)]
-        results = [keep_tile(f"result{i}", [P, X_TILES, N], F32) for i in range(O_TILES // X_TILES)]
+        results = [keep_tile(f"result{h}", [P, O_TILES, HN], F32) for h in range(2)]
         ident = keep_tile("ident", [P, P], F32)
         ident_bf = keep_tile("ident_bf", [P, P], BF16)
         dummy = keep_tile("dummy", [P, 1], F32)
@@ -79,20 +75,22 @@ def tile_soablock_pb_w4_kernel(tc, attn_bytes, attn_scale, h_x, v_w_words, v_w_s
         make_identity(nc, ident_bf[:])
         nc.scalar.activation(dummy[:], dummy[:], ACT.Identity)
 
-        def load_attn(q):
-            nc.sync.dma_start(out=codes_in[q][:], in_=attn_bytes[0, QN * q : QN * (q + 1), :].rearrange("(r j) m -> r j m", j=2))
+        def load_attn(i, first, last):
+            nc.sync.dma_start(out=codes_in[i][:], in_=attn_bytes[0, QN * first : QN * last, :].rearrange("(q r j) m -> r q j m", r=P, j=2))
+
+        def load_hx(i):
+            nc.sync.dma_start(out=hx_rows[i][:], in_=h_x[0].rearrange("(r t) m -> r t m", t=PACK)[:, 2 * i : 2 * i + 2, :])
 
         nc.sync.dma_start(
             out=scale_kp[:].rearrange("p (g t) -> p g t", t=PACK),
             in_=attn_scale.rearrange("a b (g p t) -> p (a b g) t", g=GROUPS, t=PACK),
         )
-        load_attn(0)
-        for i in range(2):
-            nc.sync.dma_start(out=hx_rows[i][:], in_=h_x[0].rearrange("(r t) m -> r t m", t=PACK)[:, 2 * i : 2 * i + 2, :])
-        load_attn(1)
+        load_attn(0, 0, 1)
+        load_hx(0)
+        load_hx(1)
+        load_attn(1, 1, 2)
         nc.sync.dma_start(out=bias_rows[0:O_TILES, :], in_=v_b.rearrange("(a p) -> a p", p=P))
-        load_attn(2)
-        load_attn(3)
+        load_attn(2, 2, 4)
         nc.sync.dma_start(out=words[:], in_=v_w_words[0])
         for r in range(4):
             nc.sync.dma_start(out=word_scales[r:P:32, :].bitcast(I32), in_=v_w_scales[0, r:16:4, :].bitcast(I32))
@@ -105,38 +103,39 @@ def tile_soablock_pb_w4_kernel(tc, attn_bytes, attn_scale, h_x, v_w_words, v_w_s
             for i in range(count):
                 nc.tensor.matmul(bank[:, 0:P], lhsT=ident[:], rhs=ident[:], start=True, stop=True)
 
-        def spread(g):
+        def spread(g, warm=False):
             bank = bank_tile()
             for t in range(PACK):
                 column = scale_kp[:, PACK * g + t : PACK * g + t + 1]
-                nc.tensor.transpose(bank[:, P * t : P * (t + 1)], column.to_broadcast([P, P]), ident[:])
+                if warm:
+                    nc.tensor.matmul(bank[:, P * t : P * (t + 1)], lhsT=column.to_broadcast([P, P]), rhs=ident[:], start=True, stop=True)
+                else:
+                    nc.tensor.transpose(bank[:, P * t : P * (t + 1)], column.to_broadcast([P, P]), ident[:])
             row = scale_row[:, K_PASS * g : K_PASS * (g + 1)].rearrange("p (k t) -> p k t", t=PACK)
             nc.scalar.copy(row, bank[:].rearrange("p (t k) -> p k t", t=PACK))
 
-        def product(q, j, first=0, last=N):
-            nc.vector.tensor_tensor(
-                out=attn_rows[q][:, j, first:last],
-                in0=codes_in[q][:, j, first:last].bitcast(F8),
-                in1=scale_row[:, first:last],
-                op=MULT,
-            )
+        def product(q, g, rows=(0, 1)):
+            codes = codes_in[min(q, 2)][:, max(q - 2, 0)]
+            cols = slice(K_PASS * g, K_PASS * (g + 1))
+            for j in rows:
+                nc.vector.tensor_tensor(out=attn_rows[q][g][:, j, :], in0=codes[:, j, cols].bitcast(F8), in1=scale_row[:, cols], op=MULT)
 
-        def turn(rows, g):
+        def turn(rows):
             bank = bank_tile()
             for j in range(2):
                 row_words = rows[:, j, :].bitcast(F32)
                 for u in range(2):
                     s = 2 * j + u
-                    nc.tensor.transpose(bank[:, P * s : P * (s + 1)], row_words[:, 256 * g + u : 256 * (g + 1) : 2], ident[:])
+                    nc.tensor.transpose(bank[:, P * s : P * (s + 1)], row_words[:, u : 2 * P : 2], ident[:])
             return bank
 
         def attn_turn(q, g):
-            bank = turn(attn_rows[q], g)
+            bank = turn(attn_rows[q][g][:])
             target = attn_kp[q][:, g, :, :].rearrange("p n t -> p (n t)").bitcast(F32)
             nc.scalar.copy(target.rearrange("p (r s) -> p r s", s=4), bank[:].rearrange("p (s r) -> p r s", s=4))
 
         def hx_turn(i, g):
-            bank = turn(hx_rows[i], g)
+            bank = turn(hx_rows[i][:, :, K_PASS * g : K_PASS * (g + 1)])
             target = hx_kp[g][:, 2 * P * i : 2 * P * (i + 1), :].rearrange("p c t -> p (c t)").bitcast(F32)
             nc.scalar.copy(target.rearrange("p (j r u) -> p j r u", j=2, u=2), bank[:].rearrange("p (j u r) -> p j r u", j=2, u=2))
 
@@ -186,95 +185,88 @@ def tile_soablock_pb_w4_kernel(tc, attn_bytes, attn_scale, h_x, v_w_words, v_w_s
                 stop=True,
             )
 
-        def finish_y(a, h, shared=False):
-            bias = bias_cols[:, a : a + 1]
-            cols = slice(HN * h, HN * (h + 1))
-            residual = xs[a // X_TILES][:, a % X_TILES, cols]
-            result = results[a // X_TILES][:, a % X_TILES, cols]
-            if shared:
-                partial = temp.tile([P, HN], F32, name="partial", tag="partial")
-                nc.scalar.activation(partial[:], y_banks[a, h][:], ACT.Identity, bias=bias)
-                nc.gpsimd.tensor_tensor(out=result, in0=partial[:], in1=residual, op=ADD)
-            else:
-                nc.vector.scalar_tensor_tensor(out=result, in0=y_banks[a, h][:], scalar=bias, in1=residual, op0=ADD, op1=ADD)
+        def residual(a, h):
+            return xs[a // X_TILES][:, a % X_TILES, HN * h : HN * (h + 1)]
+
+        def finish_y(a, h):
+            nc.vector.scalar_tensor_tensor(
+                out=results[h][:, a, :], in0=y_banks[a, h][:], scalar=bias_cols[:, a : a + 1], in1=residual(a, h), op0=ADD, op1=ADD
+            )
+
+        partials = {}
+
+        def shared_bias(a, h):
+            partials[a, h] = temp.tile([P, HN], F32, name="partial", tag=f"partial{h * (a // 4 % 2)}")
+            nc.scalar.activation(partials[a, h][:], y_banks[a, h][:], ACT.Identity, bias=bias_cols[:, a : a + 1])
+            nc.gpsimd.tensor_tensor(out=results[h][:, a, :], in0=partials[a, h][:], in1=residual(a, h), op=ADD)
 
         out_view = out.rearrange("b (a p) h w -> p a (b h w)", p=P)
 
-        def store(a, count, first=0, last=N):
-            i = a % X_TILES
-            nc.sync.dma_start(out=out_view[:, a : a + count, first:last], in_=results[a // X_TILES][:, i : i + count, first:last])
+        def store(h, first, count):
+            nc.sync.dma_start(out=out_view[:, first : first + count, HN * h : HN * (h + 1)], in_=results[h][:, first : first + count, :])
 
-        issued = [0, 0]
-
-
-        def issue_y(h, upto):
-            for a in range(issued[h], min(upto, O_TILES)):
-                y_matmul(a, h)
-                issued[h] = a + 1
-
-
-        def finish_and_store(a, h):
-            finish_y(a, h, a in SHARED[h])
-            for first, count, after in STORES[h]:
-                if after == a:
-                    store(first, count, HN * h, HN * (h + 1))
-
-
-        busy(3)
-        for g in range(GROUPS):
-            spread(g)
-            busy(1)
-        for g in range(GROUPS):
-            for j in range(2):
-                product(0, j, K_PASS * g, K_PASS * (g + 1))
-        for j in range(2):
-            product(1, j)
+        spread(0)
+        spread(1)
+        for q in range(2):
+            for g in range(GROUPS):
+                product(q, g)
         for i in range(2):
             for g in range(GROUPS):
                 hx_turn(i, g)
-                busy(1)
         attn_turn(0, 0)
+        attn_turn(0, 1)
+        attn_turn(1, 0)
         bias_turn()
-        for q, g in ((0, 1), (1, 0), (1, 1)):
-            busy(1)
-            attn_turn(q, g)
-        for g in range(GROUPS):
-            quant_hx(g)
+        attn_turn(1, 1)
+        busy(2)
+        quant_hx(0)
+        quant_hx(1)
         quant_attn(0)
-        z_quarter(0)
-        product(2, 0)
         quant_attn(1)
+        z_quarter(0)
         z_quarter(1)
+        product(2, 0)
         product(2, 1)
-        product(3, 0)
-        for g in range(GROUPS):
-            busy(1)
-            attn_turn(2, g)
         quant_z(0)
+        product(3, 0, (0,))
         quant_z(1)
-        issue_y(0, 5)
+        product(3, 0, (1,))
         product(3, 1)
+        attn_turn(2, 0)
+        attn_turn(2, 1)
 
-        for a in range(O_TILES):
-            if a == 3:
-                for g in range(GROUPS):
-                    attn_turn(3, g)
-            elif a == 4:
-                quant_attn(2)
-            elif a == 6:
-                quant_attn(3)
-            elif a == 9:
-                z_quarter(2)
-            elif a == 12:
-                z_quarter(3)
-            elif a == 13:
-                quant_z(2)
-            elif a == 15:
-                quant_z(3)
-            if a >= 3:
-                issue_y(0, a + 4)
-            finish_and_store(a, 0)
+        def y_round(r, h):
+            y_matmul(4 * r + 3, h)
+            shared_bias(4 * r + 3, h)
+            for a in range(4 * r, 4 * r + 3):
+                y_matmul(a, h)
 
-        for a in range(O_TILES):
-            issue_y(1, a + 6)
-            finish_and_store(a, 1)
+        def finish_round(r, h, sizes):
+            first = 4 * r
+            for size in sizes:
+                for a in range(first, min(first + size, 4 * r + 3)):
+                    finish_y(a, h)
+                store(h, first, size)
+                first = first + size
+
+        y_round(0, 0)
+        attn_turn(3, 0)
+        attn_turn(3, 1)
+        finish_round(0, 0, (1, 1, 2))
+        y_round(1, 0)
+        quant_attn(2)
+        z_quarter(2)
+        finish_round(1, 0, (1, 1, 2))
+        y_round(2, 0)
+        quant_attn(3)
+        z_quarter(3)
+        finish_round(2, 0, (1, 1, 2))
+        y_round(3, 0)
+        quant_z(2)
+        quant_z(3)
+        finish_round(3, 0, (1, 1, 2))
+        y_round(0, 1)
+        for r in range(4):
+            if r < 3:
+                y_round(r + 1, 1)
+            finish_round(r, 1, SIZES[r])

@@ -111,31 +111,37 @@ def tile_soablock_pb_w4_kernel(tc, attn_bytes, attn_scale, h_x, v_w_words, v_w_s
                     nc.tensor.matmul(bank[:, P * t : P * (t + 1)], lhsT=column.to_broadcast([P, P]), rhs=ident[:], start=True, stop=True)
                 else:
                     nc.tensor.transpose(bank[:, P * t : P * (t + 1)], column.to_broadcast([P, P]), ident[:])
-            row = scale_row[:, K_PASS * g : K_PASS * (g + 1)].rearrange("p (k t) -> p k t", t=PACK)
-            nc.scalar.copy(row, bank[:].rearrange("p (t k) -> p k t", t=PACK))
+            row = scale_row[:, K_PASS * g : K_PASS * (g + 1)].rearrange("p (u k e) -> p u k e", u=2, e=2)
+            nc.scalar.copy(row, bank[:].rearrange("p (u e k) -> p u k e", u=2, e=2))
 
         def product(q, g, rows=(0, 1)):
             codes = codes_in[min(q, 2)][:, max(q - 2, 0)]
             cols = slice(K_PASS * g, K_PASS * (g + 1))
             for j in rows:
-                nc.vector.tensor_tensor(out=attn_rows[q][g][:, j, :], in0=codes[:, j, cols].bitcast(F8), in1=scale_row[:, cols], op=MULT)
+                nc.vector.tensor_tensor(
+                    out=attn_rows[q][g][:, j, :].rearrange("p (u k e) -> p u k e", u=2, e=2),
+                    in0=codes[:, j, cols].bitcast(F8).rearrange("p (k u e) -> p u k e", u=2, e=2),
+                    in1=scale_row[:, cols].rearrange("p (u k e) -> p u k e", u=2, e=2),
+                    op=MULT,
+                )
 
-        def turn(rows):
+        def turn(rows, is_sorted):
             bank = bank_tile()
             for j in range(2):
                 row_words = rows[:, j, :].bitcast(F32)
                 for u in range(2):
                     s = 2 * j + u
-                    nc.tensor.transpose(bank[:, P * s : P * (s + 1)], row_words[:, u : 2 * P : 2], ident[:])
+                    run = row_words[:, P * u : P * (u + 1)] if is_sorted else row_words[:, u : 2 * P : 2]
+                    nc.tensor.transpose(bank[:, P * s : P * (s + 1)], run, ident[:])
             return bank
 
         def attn_turn(q, g):
-            bank = turn(attn_rows[q][g][:])
+            bank = turn(attn_rows[q][g][:], True)
             target = attn_kp[q][:, g, :, :].rearrange("p n t -> p (n t)").bitcast(F32)
             nc.scalar.copy(target.rearrange("p (r s) -> p r s", s=4), bank[:].rearrange("p (s r) -> p r s", s=4))
 
         def hx_turn(i, g):
-            bank = turn(hx_rows[i][:, :, K_PASS * g : K_PASS * (g + 1)])
+            bank = turn(hx_rows[i][:, :, K_PASS * g : K_PASS * (g + 1)], False)
             target = hx_kp[g][:, 2 * P * i : 2 * P * (i + 1), :].rearrange("p c t -> p (c t)").bitcast(F32)
             nc.scalar.copy(target.rearrange("p (j r u) -> p j r u", j=2, u=2), bank[:].rearrange("p (j u r) -> p j r u", j=2, u=2))
 

@@ -27,7 +27,7 @@ O_TILES = C // P
 X_TILES = 8
 FLOPS = 2 * MID * N * N + 2 * C * MID * N
 
-SIZES = ((2, 2), (2, 2), (4,), (4,))
+STORES = {1: (0, 2), 2: (2, 2), 6: (4, 4), 10: (8, 4), 14: (12, 4)}
 
 
 def tile_soablock_pb_w4_kernel(tc, attn_bytes, attn_scale, h_x, v_w_words, v_w_scales, v_b, x, out):
@@ -202,7 +202,7 @@ def tile_soablock_pb_w4_kernel(tc, attn_bytes, attn_scale, h_x, v_w_words, v_w_s
         partials = {}
 
         def shared_bias(a, h):
-            partials[a, h] = temp.tile([P, HN], F32, name="partial", tag=f"partial{h * (a // 4 % 2)}")
+            partials[a, h] = temp.tile([P, HN], F32, name="partial", tag=f"partial{h * (1 - a // 4 % 2)}")
             nc.scalar.activation(partials[a, h][:], y_banks[a, h][:], ACT.Identity, bias=bias_cols[:, a : a + 1])
             nc.gpsimd.tensor_tensor(out=results[h][:, a, :], in0=partials[a, h][:], in1=residual(a, h), op=ADD)
 
@@ -265,14 +265,26 @@ def tile_soablock_pb_w4_kernel(tc, attn_bytes, attn_scale, h_x, v_w_words, v_w_s
         finish_round(1, 0, (1, 1, 2))
         y_round(2, 0)
         quant_attn(3)
+        y_matmul(12, 0)
         z_quarter(3)
         finish_round(2, 0, (1, 1, 2))
-        y_round(3, 0)
+        y_matmul(15, 0)
+        shared_bias(15, 0)
+        y_matmul(13, 0)
+        y_matmul(14, 0)
+        finish_y(12, 0)
+        store(0, 12, 1)
         quant_z(2)
         quant_z(3)
-        finish_round(3, 0, (1, 1, 2))
+        finish_y(13, 0)
+        store(0, 13, 1)
+        finish_y(14, 0)
+        store(0, 14, 2)
         y_round(0, 1)
         for r in range(4):
             if r < 3:
                 y_round(r + 1, 1)
-            finish_round(r, 1, SIZES[r])
+            for a in range(4 * r, 4 * r + 3):
+                finish_y(a, 1)
+                if a in STORES:
+                    store(1, *STORES[a])

@@ -39,7 +39,7 @@ def tile_soablock_pb_w4_kernel(tc, attn_bytes, attn_scale, h_x, v_w_words, v_w_s
         ctx.enter_context(tc.manual_schedule())
 
         def keep_tile(name, shape, dtype):
-            return keep.tile(shape, dtype, name=name, tag=name, align_bytes=64)
+            return keep.tile(shape, dtype, name=name, tag=name, align_bytes=256)
 
         def bank_tile():
             return psum.tile([P, HN], F32, name="bank", tag="bank")
@@ -202,7 +202,7 @@ def tile_soablock_pb_w4_kernel(tc, attn_bytes, attn_scale, h_x, v_w_words, v_w_s
         partials = {}
 
         def shared_bias(a, h):
-            partials[a, h] = temp.tile([P, HN], F32, name="partial", tag=f"partial{h * (1 - a // 4 % 2)}")
+            partials[a, h] = temp.tile([P, HN], F32, name="partial", tag=f"partial{h * (1 - a // 4 % 2)}", align_bytes=256)
             nc.scalar.activation(partials[a, h][:], y_banks[a, h][:], ACT.Identity, bias=bias_cols[:, a : a + 1])
             nc.gpsimd.tensor_tensor(out=results[h][:, a, :], in0=partials[a, h][:], in1=residual(a, h), op=ADD)
 

@@ -27,7 +27,7 @@ O_TILES = C // P
 X_TILES = 8
 FLOPS = 2 * MID * N * N + 2 * C * MID * N
 
-STORES = {1: (0, 2), 2: (2, 2), 6: (4, 4), 10: (8, 4), 14: (12, 4)}
+ROUND = 4
 
 
 def tile_soablock_pb_w4_kernel(tc, attn_bytes, attn_scale, h_x, v_w_words, v_w_scales, v_b, x, out):
@@ -103,14 +103,11 @@ def tile_soablock_pb_w4_kernel(tc, attn_bytes, attn_scale, h_x, v_w_words, v_w_s
             for i in range(count):
                 nc.tensor.matmul(bank[:, 0:P], lhsT=ident[:], rhs=ident[:], start=True, stop=True)
 
-        def spread(g, warm=False):
+        def spread(g):
             bank = bank_tile()
             for t in range(PACK):
                 column = scale_kp[:, PACK * g + t : PACK * g + t + 1]
-                if warm:
-                    nc.tensor.matmul(bank[:, P * t : P * (t + 1)], lhsT=column.to_broadcast([P, P]), rhs=ident[:], start=True, stop=True)
-                else:
-                    nc.tensor.transpose(bank[:, P * t : P * (t + 1)], column.to_broadcast([P, P]), ident[:])
+                nc.tensor.transpose(bank[:, P * t : P * (t + 1)], column.to_broadcast([P, P]), ident[:])
             row = scale_row[:, K_PASS * g : K_PASS * (g + 1)].rearrange("p (u k e) -> p u k e", u=2, e=2)
             nc.scalar.copy(row, bank[:].rearrange("p (u e k) -> p u k e", u=2, e=2))
 
@@ -191,6 +188,20 @@ def tile_soablock_pb_w4_kernel(tc, attn_bytes, attn_scale, h_x, v_w_words, v_w_s
                 stop=True,
             )
 
+        def y_quarter(a, q):
+            if q == 0:
+                y_banks[a, 0] = bank_tile()
+            cols = slice(QN * q, QN * (q + 1))
+            nc.tensor.matmul_mx(
+                out=y_banks[a, 0][:, cols],
+                lhsT=words[:, 2 * P * a : 2 * P * (a + 1)].bitcast(FP4X4),
+                lhsT_scale=word_scales[:, P * a : P * (a + 1)],
+                rhs=z_codes[0][:, cols].bitcast(FP8X4),
+                rhs_scale=z_scales[0][:, cols],
+                start=True,
+                stop=True,
+            )
+
         def residual(a, h):
             return xs[a // X_TILES][:, a % X_TILES, HN * h : HN * (h + 1)]
 
@@ -211,6 +222,20 @@ def tile_soablock_pb_w4_kernel(tc, attn_bytes, attn_scale, h_x, v_w_words, v_w_s
         def store(h, first, count):
             nc.sync.dma_start(out=out_view[:, first : first + count, HN * h : HN * (h + 1)], in_=results[h][:, first : first + count, :])
 
+        def y_round(r, h):
+            y_matmul(4 * r + 3, h)
+            shared_bias(4 * r + 3, h)
+            for a in range(4 * r, 4 * r + 3):
+                y_matmul(a, h)
+
+        def finish_round(r, h, sizes):
+            first = 4 * r
+            for size in sizes:
+                for a in range(first, min(first + size, 4 * r + 3)):
+                    finish_y(a, h)
+                store(h, first, size)
+                first = first + size
+
         spread(0)
         spread(1)
         for q in range(2):
@@ -228,63 +253,47 @@ def tile_soablock_pb_w4_kernel(tc, attn_bytes, attn_scale, h_x, v_w_words, v_w_s
         quant_hx(0)
         quant_hx(1)
         quant_attn(0)
+        product(2, 0)
         quant_attn(1)
         z_quarter(0)
         z_quarter(1)
-        product(2, 0)
         product(2, 1)
-        quant_z(0)
         product(3, 0, (0,))
-        quant_z(1)
+        quant_z(0)
         product(3, 0, (1,))
+        quant_z(1)
         product(3, 1)
         attn_turn(2, 0)
         attn_turn(2, 1)
-
-        def y_round(r, h):
-            y_matmul(4 * r + 3, h)
-            shared_bias(4 * r + 3, h)
-            for a in range(4 * r, 4 * r + 3):
-                y_matmul(a, h)
-
-        def finish_round(r, h, sizes):
-            first = 4 * r
-            for size in sizes:
-                for a in range(first, min(first + size, 4 * r + 3)):
-                    finish_y(a, h)
-                store(h, first, size)
-                first = first + size
-
-        y_round(0, 0)
+        for q in range(2):
+            for a in (3, 0, 1, 2):
+                y_quarter(a, q)
+        shared_bias(3, 0)
         attn_turn(3, 0)
         attn_turn(3, 1)
         finish_round(0, 0, (1, 1, 2))
         y_round(1, 0)
         quant_attn(2)
         z_quarter(2)
-        finish_round(1, 0, (1, 1, 2))
+        finish_round(1, 0, (2, 2))
         y_round(2, 0)
         quant_attn(3)
         y_matmul(12, 0)
         z_quarter(3)
-        finish_round(2, 0, (1, 1, 2))
+        finish_round(2, 0, (2, 2))
         y_matmul(15, 0)
         shared_bias(15, 0)
         y_matmul(13, 0)
         y_matmul(14, 0)
         finish_y(12, 0)
-        store(0, 12, 1)
         quant_z(2)
         quant_z(3)
         finish_y(13, 0)
-        store(0, 13, 1)
+        store(0, 12, 2)
         finish_y(14, 0)
         store(0, 14, 2)
         y_round(0, 1)
-        for r in range(4):
-            if r < 3:
+        for r, sizes in enumerate(((4,), (4,), (4,), (4,))):
+            if r + 1 < O_TILES // ROUND:
                 y_round(r + 1, 1)
-            for a in range(4 * r, 4 * r + 3):
-                finish_y(a, 1)
-                if a in STORES:
-                    store(1, *STORES[a])
+            finish_round(r, 1, sizes)

@@ -45,9 +45,10 @@ def tile_soablock_pb_w4_kernel(tc, attn_bytes, attn_scale, h_x, v_w_words, v_w_s
             return psum.tile([P, HN], F32, name="bank", tag="bank")
 
         scale_kp = keep_tile("scale_kp", [P, GROUPS * PACK], F32)
+        scale_groups = keep_tile("scale_groups", [P, N], F32)
         scale_row = keep_tile("scale_row", [P, N], F32)
         codes_in = [keep_tile(f"codes_in{i}", [P, count, 2, N], U8) for i, count in enumerate((1, 1, 2))]
-        attn_rows = [[keep_tile(f"attn_rows{q}_{g}", [P, 2, K_PASS], BF16) for g in range(GROUPS)] for q in range(QUARTERS)]
+        attn_rows = [[keep_tile(f"attn_rows{q}_{j}", [P, N], BF16) for j in range(2)] for q in range(QUARTERS)]
         hx_rows = [keep_tile(f"hx_rows{i}", [P, 2, N], BF16) for i in range(2)]
         words = keep_tile("words", [P, 2 * C], U8)
         word_scales = keep_tile("word_scales", [P, C], U8)
@@ -60,7 +61,7 @@ def tile_soablock_pb_w4_kernel(tc, attn_bytes, attn_scale, h_x, v_w_words, v_w_s
         hx_kp = [keep_tile(f"hx_kp{g}", [P, MID, PACK], BF16) for g in range(GROUPS)]
         hx_codes = [keep_tile(f"hx_codes{g}", [P, MID], U32) for g in range(GROUPS)]
         hx_scales = [keep_tile(f"hx_scales{g}", [P, MID], U8) for g in range(GROUPS)]
-        z_kp = [keep_tile(f"z_kp{q}", [P, QN, PACK], BF16) for q in range(QUARTERS)]
+        z_kp = [keep_tile(f"z_kp{h}", [P, HN, PACK], BF16) for h in range(2)]
         z_codes = [keep_tile(f"z_codes{h}", [P, HN], U32) for h in range(2)]
         z_scales = [keep_tile(f"z_scales{h}", [P, HN], U8) for h in range(2)]
         results = [keep_tile(f"result{h}", [P, O_TILES, HN], F32) for h in range(2)]
@@ -87,8 +88,8 @@ def tile_soablock_pb_w4_kernel(tc, attn_bytes, attn_scale, h_x, v_w_words, v_w_s
         )
         load_attn(0, 0, 1)
         load_hx(0)
-        load_hx(1)
         load_attn(1, 1, 2)
+        load_hx(1)
         nc.sync.dma_start(out=bias_rows[0:O_TILES, :], in_=v_b.rearrange("(a p) -> a p", p=P))
         load_attn(2, 2, 4)
         nc.sync.dma_start(out=words[:], in_=v_w_words[0])
@@ -103,42 +104,60 @@ def tile_soablock_pb_w4_kernel(tc, attn_bytes, attn_scale, h_x, v_w_words, v_w_s
             for i in range(count):
                 nc.tensor.matmul(bank[:, 0:P], lhsT=ident[:], rhs=ident[:], start=True, stop=True)
 
-        def spread(g):
-            bank = bank_tile()
-            for t in range(PACK):
-                column = scale_kp[:, PACK * g + t : PACK * g + t + 1]
-                nc.tensor.transpose(bank[:, P * t : P * (t + 1)], column.to_broadcast([P, P]), ident[:])
-            row = scale_row[:, K_PASS * g : K_PASS * (g + 1)].rearrange("p (u k e) -> p u k e", u=2, e=2)
-            nc.scalar.copy(row, bank[:].rearrange("p (u e k) -> p u k e", u=2, e=2))
+        spread_banks = {}
 
-        def product(q, g, rows=(0, 1)):
-            codes = codes_in[min(q, 2)][:, max(q - 2, 0)]
-            cols = slice(K_PASS * g, K_PASS * (g + 1))
-            for j in rows:
+        def spread(g, words_u):
+            bank = bank_tile()
+            width = 2 * P * len(words_u)
+            for s in range(2 * len(words_u)):
+                t = 2 * words_u[0] + s
+                column = scale_kp[:, PACK * g + t : PACK * g + t + 1]
+                nc.tensor.transpose(bank[:, P * s : P * (s + 1)], column.to_broadcast([P, P]), ident[:])
+            spread_banks[g, words_u] = bank[:, 0:width].rearrange("p (u e k) -> p u k e", e=2, k=P)
+            first = K_PASS * g + 2 * P * words_u[0]
+            nc.scalar.copy(scale_groups[:, first : first + width].rearrange("p (u k e) -> p u k e", e=2, k=P), spread_banks[g, words_u])
+
+        def fill_scale_row():
+            for (g, words_u), bank in spread_banks.items():
+                target = scale_row[:].rearrange("p (u g k e) -> p u g k e", u=2, g=GROUPS, e=2)
+                nc.scalar.copy(target[:, words_u[0] : words_u[-1] + 1, g], bank)
+
+        def row_codes(q, j):
+            return codes_in[min(q, 2)][:, max(q - 2, 0), j, :].bitcast(F8)
+
+        def first_product(g, words_u):
+            cols = slice(K_PASS * g + 2 * P * words_u[0], K_PASS * g + 2 * P * (words_u[-1] + 1))
+            for j in range(2):
+                codes = row_codes(0, j)[:, K_PASS * g : K_PASS * (g + 1)].rearrange("p (k u e) -> p u k e", u=2, e=2)
                 nc.vector.tensor_tensor(
-                    out=attn_rows[q][g][:, j, :].rearrange("p (u k e) -> p u k e", u=2, e=2),
-                    in0=codes[:, j, cols].bitcast(F8).rearrange("p (k u e) -> p u k e", u=2, e=2),
-                    in1=scale_row[:, cols].rearrange("p (u k e) -> p u k e", u=2, e=2),
+                    out=attn_rows[0][j][:, cols].rearrange("p (u k e) -> p u k e", e=2, k=P),
+                    in0=codes[:, words_u[0] : words_u[-1] + 1],
+                    in1=scale_groups[:, cols].rearrange("p (u k e) -> p u k e", e=2, k=P),
                     op=MULT,
                 )
 
-        def turn(rows, is_sorted):
+        def product(q, j):
+            nc.vector.tensor_tensor(
+                out=attn_rows[q][j][:].rearrange("p (u k e) -> p u k e", u=2, e=2),
+                in0=row_codes(q, j).rearrange("p (k u e) -> p u k e", u=2, e=2),
+                in1=scale_row[:].rearrange("p (u k e) -> p u k e", u=2, e=2),
+                op=MULT,
+            )
+
+        def turn(runs):
             bank = bank_tile()
-            for j in range(2):
-                row_words = rows[:, j, :].bitcast(F32)
-                for u in range(2):
-                    s = 2 * j + u
-                    run = row_words[:, P * u : P * (u + 1)] if is_sorted else row_words[:, u : 2 * P : 2]
-                    nc.tensor.transpose(bank[:, P * s : P * (s + 1)], run, ident[:])
+            for s, run in enumerate(runs):
+                nc.tensor.transpose(bank[:, P * s : P * (s + 1)], run, ident[:])
             return bank
 
         def attn_turn(q, g):
-            bank = turn(attn_rows[q][g][:], True)
+            firsts = [P * (2 * g + u if q == 0 else 2 * u + g) for u in range(2)]
+            bank = turn([attn_rows[q][j][:].bitcast(F32)[:, first : first + P] for j in range(2) for first in firsts])
             target = attn_kp[q][:, g, :, :].rearrange("p n t -> p (n t)").bitcast(F32)
             nc.scalar.copy(target.rearrange("p (r s) -> p r s", s=4), bank[:].rearrange("p (s r) -> p r s", s=4))
 
         def hx_turn(i, g):
-            bank = turn(hx_rows[i][:, :, K_PASS * g : K_PASS * (g + 1)], False)
+            bank = turn([hx_rows[i][:, tt, :].bitcast(F32)[:, 2 * P * g + u : 2 * P * (g + 1) : 2] for tt in range(2) for u in range(2)])
             target = hx_kp[g][:, 2 * P * i : 2 * P * (i + 1), :].rearrange("p c t -> p (c t)").bitcast(F32)
             nc.scalar.copy(target.rearrange("p (j r u) -> p j r u", j=2, u=2), bank[:].rearrange("p (j u r) -> p j r u", j=2, u=2))
 
@@ -168,11 +187,10 @@ def tile_soablock_pb_w4_kernel(tc, attn_bytes, attn_scale, h_x, v_w_words, v_w_s
                             start=(g == 0),
                             stop=(g == GROUPS - 1),
                         )
-                nc.scalar.copy(z_kp[q][:, P * part : P * (part + 1), :], bank[:].rearrange("p (t n) -> p n t", t=PACK))
+                nc.scalar.copy(z_kp[q // 2][:, QN * (q % 2) + P * part : QN * (q % 2) + P * (part + 1), :], bank[:].rearrange("p (t n) -> p n t", t=PACK))
 
-        def quant_z(q):
-            h, cols = q // 2, slice(QN * (q % 2), QN * (q % 2 + 1))
-            nc.vector.quantize_mx(out=z_codes[h][:, cols].bitcast(FP8X4), scales=z_scales[h][:, cols], in_=z_kp[q][:].rearrange("p n t -> p (n t)"))
+        def quant_z(h, cols):
+            nc.vector.quantize_mx(out=z_codes[h][:, cols].bitcast(FP8X4), scales=z_scales[h][:, cols], in_=z_kp[h][:, cols, :].rearrange("p n t -> p (n t)"))
 
         y_banks = {}
 
@@ -236,11 +254,15 @@ def tile_soablock_pb_w4_kernel(tc, attn_bytes, attn_scale, h_x, v_w_words, v_w_s
                 store(h, first, size)
                 first = first + size
 
-        spread(0)
-        spread(1)
-        for q in range(2):
-            for g in range(GROUPS):
-                product(q, g)
+        spread(0, (0,))
+        spread(0, (1,))
+        spread(1, (0, 1))
+        fill_scale_row()
+        first_product(0, (0,))
+        first_product(0, (1,))
+        first_product(1, (0, 1))
+        product(1, 0)
+        product(1, 1)
         for i in range(2):
             for g in range(GROUPS):
                 hx_turn(i, g)
@@ -258,10 +280,9 @@ def tile_soablock_pb_w4_kernel(tc, attn_bytes, attn_scale, h_x, v_w_words, v_w_s
         z_quarter(0)
         z_quarter(1)
         product(2, 1)
-        product(3, 0, (0,))
-        quant_z(0)
-        product(3, 0, (1,))
-        quant_z(1)
+        quant_z(0, slice(0, QN))
+        product(3, 0)
+        quant_z(0, slice(QN, HN))
         product(3, 1)
         attn_turn(2, 0)
         attn_turn(2, 1)
@@ -275,25 +296,25 @@ def tile_soablock_pb_w4_kernel(tc, attn_bytes, attn_scale, h_x, v_w_words, v_w_s
         y_round(1, 0)
         quant_attn(2)
         z_quarter(2)
-        finish_round(1, 0, (2, 2))
+        finish_round(1, 0, (1, 1, 2))
         y_round(2, 0)
         quant_attn(3)
         y_matmul(12, 0)
         z_quarter(3)
-        finish_round(2, 0, (2, 2))
+        finish_round(2, 0, (1, 1, 2))
         y_matmul(15, 0)
         shared_bias(15, 0)
         y_matmul(13, 0)
         y_matmul(14, 0)
         finish_y(12, 0)
-        quant_z(2)
-        quant_z(3)
+        store(0, 12, 1)
+        quant_z(1, slice(0, HN))
         finish_y(13, 0)
-        store(0, 12, 2)
+        store(0, 13, 1)
         finish_y(14, 0)
         store(0, 14, 2)
         y_round(0, 1)
-        for r, sizes in enumerate(((4,), (4,), (4,), (4,))):
+        for r, sizes in enumerate(((2, 2), (4,), (4,), (4,))):
             if r + 1 < O_TILES // ROUND:
                 y_round(r + 1, 1)
             finish_round(r, 1, sizes)

@@ -68,7 +68,9 @@ def tile_soablock_pb_w4_kernel(tc, attn_bytes, attn_scale, h_x, v_w_words, v_w_s
         ident = keep_tile("ident", [P, P], F32)
         ident_bf = keep_tile("ident_bf", [P, P], BF16)
         dummy = keep_tile("dummy", [P, 1], F32)
+        zeros = keep_tile("zeros", [P, P], F32)
 
+        nc.gpsimd.memset(zeros[:], 0.0)
         nc.vector.memset(dummy[:], 0.0)
         nc.vector.memset(bias_rows[:], 0.0)
         nc.vector.memset(word_scales[:].bitcast(I32), 0)
@@ -103,6 +105,10 @@ def tile_soablock_pb_w4_kernel(tc, attn_bytes, attn_scale, h_x, v_w_words, v_w_s
             bank = bank_tile()
             for i in range(count):
                 nc.tensor.matmul(bank[:, 0:P], lhsT=ident[:], rhs=ident[:], start=True, stop=True)
+
+        def warm(repeats):
+            target = bank_tile()[:, 0 : P * repeats].rearrange("p (r c) -> p r c", c=P)
+            nc.tensor.matmul(target, lhsT=zeros[:], rhs=zeros[:].unsqueeze(1).to_broadcast([P, repeats, P]), start=True, stop=True)
 
         spread_banks = {}
 
@@ -254,9 +260,11 @@ def tile_soablock_pb_w4_kernel(tc, attn_bytes, attn_scale, h_x, v_w_words, v_w_s
                 store(h, first, size)
                 first = first + size
 
+        warm(3)
         spread(0, (0,))
         spread(0, (1,))
         spread(1, (0, 1))
+        warm(2)
         fill_scale_row()
         first_product(0, (0,))
         first_product(0, (1,))

from contextlib import ExitStack

import concourse.mybir as mybir
from concourse.masks import make_identity

F32 = mybir.dt.float32
BF16 = mybir.dt.bfloat16
I32 = mybir.dt.int32
U32 = mybir.dt.uint32
U8 = mybir.dt.uint8
F8 = mybir.dt.float8_e4m3fn
FP8X4 = mybir.dt.float8_e4m3fn_x4
FP4X4 = mybir.dt.float4_e2m1fn_x4
MULT = mybir.AluOpType.mult
ADD = mybir.AluOpType.add
ACT = mybir.ActivationFunctionType

P = 128
PACK = 4
K_PASS = P * PACK
C, MID, N = 2048, 512, 1024
GROUPS = N // K_PASS
QUARTERS = 4
QN = N // QUARTERS
HN = N // 2
O_TILES = C // P
X_TILES = 8
FLOPS = 2 * MID * N * N + 2 * C * MID * N

ROUND = 4


def tile_soablock_pb_w4_kernel(tc, attn_bytes, attn_scale, h_x, v_w_words, v_w_scales, v_b, x, out):
    nc = tc.nc
    with ExitStack() as ctx:
        keep = ctx.enter_context(tc.tile_pool(name="keep", bufs=1))
        temp = ctx.enter_context(tc.tile_pool(name="temp", bufs=1))
        psum = ctx.enter_context(tc.psum_pool(name="psum", bufs=8))
        ctx.enter_context(tc.manual_schedule())

        def keep_tile(name, shape, dtype):
            return keep.tile(shape, dtype, name=name, tag=name, align_bytes=256)

        def bank_tile():
            return psum.tile([P, HN], F32, name="bank", tag="bank")

        scale_kp = keep_tile("scale_kp", [P, GROUPS * PACK], F32)
        scale_groups = keep_tile("scale_groups", [P, N], F32)
        scale_row = keep_tile("scale_row", [P, N], F32)
        codes_in = [keep_tile(f"codes_in{i}", [P, count, 2, N], U8) for i, count in enumerate((1, 1, 2))]
        attn_rows = [[keep_tile(f"attn_rows{q}_{j}", [P, N], BF16) for j in range(2)] for q in range(QUARTERS)]
        hx_rows = [keep_tile(f"hx_rows{i}", [P, 2, N], BF16) for i in range(2)]
        words = keep_tile("words", [P, 2 * C], U8)
        word_scales = keep_tile("word_scales", [P, C], U8)
        bias_rows = keep_tile("bias_rows", [P, P], BF16)
        bias_cols = keep_tile("bias_cols", [P, O_TILES], F32)
        xs = [keep_tile(f"xs{i}", [P, X_TILES, N], BF16) for i in range(O_TILES // X_TILES)]
        attn_kp = [keep_tile(f"attn_kp{q}", [P, GROUPS, QN, PACK], BF16) for q in range(QUARTERS)]
        attn_codes = [keep_tile(f"attn_codes{q}", [P, GROUPS * QN], U32) for q in range(QUARTERS)]
        attn_scales = [keep_tile(f"attn_scales{q}", [P, GROUPS * QN], U8) for q in range(QUARTERS)]
        hx_kp = [keep_tile(f"hx_kp{g}", [P, MID, PACK], BF16) for g in range(GROUPS)]
        hx_codes = [keep_tile(f"hx_codes{g}", [P, MID], U32) for g in range(GROUPS)]
        hx_scales = [keep_tile(f"hx_scales{g}", [P, MID], U8) for g in range(GROUPS)]
        z_kp = [keep_tile(f"z_kp{h}", [P, HN, PACK], BF16) for h in range(2)]
        z_codes = [keep_tile(f"z_codes{h}", [P, HN], U32) for h in range(2)]
        z_scales = [keep_tile(f"z_scales{h}", [P, HN], U8) for h in range(2)]
        results = [keep_tile(f"result{h}", [P, O_TILES, HN], F32) for h in range(2)]
        ident = keep_tile("ident", [P, P], F32)
        ident_bf = keep_tile("ident_bf", [P, P], BF16)
        dummy = keep_tile("dummy", [P, 1], F32)
        zeros = keep_tile("zeros", [P, P], F32)

        nc.gpsimd.memset(zeros[:], 0.0)
        nc.vector.memset(dummy[:], 0.0)
        nc.vector.memset(bias_rows[:], 0.0)
        nc.vector.memset(word_scales[:].bitcast(I32), 0)
        make_identity(nc, ident[:])
        make_identity(nc, ident_bf[:])
        nc.scalar.activation(dummy[:], dummy[:], ACT.Identity)

        def load_attn(i, first, last):
            nc.sync.dma_start(out=codes_in[i][:], in_=attn_bytes[0, QN * first : QN * last, :].rearrange("(q r j) m -> r q j m", r=P, j=2))

        def load_hx(i):
            nc.sync.dma_start(out=hx_rows[i][:], in_=h_x[0].rearrange("(r t) m -> r t m", t=PACK)[:, 2 * i : 2 * i + 2, :])

        nc.sync.dma_start(
            out=scale_kp[:].rearrange("p (g t) -> p g t", t=PACK),
            in_=attn_scale.rearrange("a b (g p t) -> p (a b g) t", g=GROUPS, t=PACK),
        )
        load_attn(0, 0, 1)
        load_hx(0)
        load_attn(1, 1, 2)
        load_hx(1)
        nc.sync.dma_start(out=bias_rows[0:O_TILES, :], in_=v_b.rearrange("(a p) -> a p", p=P))
        load_attn(2, 2, 4)
        nc.sync.dma_start(out=words[:], in_=v_w_words[0])
        for r in range(4):
            nc.sync.dma_start(out=word_scales[r:P:32, :].bitcast(I32), in_=v_w_scales[0, r:16:4, :].bitcast(I32))
        x_view = x.rearrange("b (a p) h w -> p a (b h w)", p=P)
        for i in range(O_TILES // X_TILES):
            nc.sync.dma_start(out=xs[i][:], in_=x_view[:, X_TILES * i : X_TILES * (i + 1), :])

        def busy(count):
            bank = bank_tile()
            for i in range(count):
                nc.tensor.matmul(bank[:, 0:P], lhsT=ident[:], rhs=ident[:], start=True, stop=True)

        def warm(repeats):
            target = bank_tile()[:, 0 : P * repeats].rearrange("p (r c) -> p r c", c=P)
            nc.tensor.matmul(target, lhsT=zeros[:], rhs=zeros[:].unsqueeze(1).to_broadcast([P, repeats, P]), start=True, stop=True)

        spread_banks = {}

        def spread(g, words_u):
            bank = bank_tile()
            width = 2 * P * len(words_u)
            for s in range(2 * len(words_u)):
                t = 2 * words_u[0] + s
                column = scale_kp[:, PACK * g + t : PACK * g + t + 1]
                nc.tensor.transpose(bank[:, P * s : P * (s + 1)], column.to_broadcast([P, P]), ident[:])
            spread_banks[g, words_u] = bank[:, 0:width].rearrange("p (u e k) -> p u k e", e=2, k=P)
            first = K_PASS * g + 2 * P * words_u[0]
            nc.scalar.copy(scale_groups[:, first : first + width].rearrange("p (u k e) -> p u k e", e=2, k=P), spread_banks[g, words_u])

        def fill_scale_row():
            for (g, words_u), bank in spread_banks.items():
                target = scale_row[:].rearrange("p (u g k e) -> p u g k e", u=2, g=GROUPS, e=2)
                nc.scalar.copy(target[:, words_u[0] : words_u[-1] + 1, g], bank)

        def row_codes(q, j):
            return codes_in[min(q, 2)][:, max(q - 2, 0), j, :].bitcast(F8)

        def first_product(g, words_u):
            cols = slice(K_PASS * g + 2 * P * words_u[0], K_PASS * g + 2 * P * (words_u[-1] + 1))
            for j in range(2):
                codes = row_codes(0, j)[:, K_PASS * g : K_PASS * (g + 1)].rearrange("p (k u e) -> p u k e", u=2, e=2)
                nc.vector.tensor_tensor(
                    out=attn_rows[0][j][:, cols].rearrange("p (u k e) -> p u k e", e=2, k=P),
                    in0=codes[:, words_u[0] : words_u[-1] + 1],
                    in1=scale_groups[:, cols].rearrange("p (u k e) -> p u k e", e=2, k=P),
                    op=MULT,
                )

        def product(q, j):
            nc.vector.tensor_tensor(
                out=attn_rows[q][j][:].rearrange("p (u k e) -> p u k e", u=2, e=2),
                in0=row_codes(q, j).rearrange("p (k u e) -> p u k e", u=2, e=2),
                in1=scale_row[:].rearrange("p (u k e) -> p u k e", u=2, e=2),
                op=MULT,
            )

        def turn(runs):
            bank = bank_tile()
            for s, run in enumerate(runs):
                nc.tensor.transpose(bank[:, P * s : P * (s + 1)], run, ident[:])
            return bank

        def attn_turn(q, g):
            firsts = [P * (2 * g + u if q == 0 else 2 * u + g) for u in range(2)]
            bank = turn([attn_rows[q][j][:].bitcast(F32)[:, first : first + P] for j in range(2) for first in firsts])
            target = attn_kp[q][:, g, :, :].rearrange("p n t -> p (n t)").bitcast(F32)
            nc.scalar.copy(target.rearrange("p (r s) -> p r s", s=4), bank[:].rearrange("p (s r) -> p r s", s=4))

        def hx_turn(i, g):
            bank = turn([hx_rows[i][:, tt, :].bitcast(F32)[:, 2 * P * g + u : 2 * P * (g + 1) : 2] for tt in range(2) for u in range(2)])
            target = hx_kp[g][:, 2 * P * i : 2 * P * (i + 1), :].rearrange("p c t -> p (c t)").bitcast(F32)
            nc.scalar.copy(target.rearrange("p (j r u) -> p j r u", j=2, u=2), bank[:].rearrange("p (j u r) -> p j r u", j=2, u=2))

        def bias_turn():
            bank = psum.tile([P, P], BF16, name="bank", tag="bank")
            nc.tensor.transpose(bank[:], bias_rows[:], ident_bf[:])
            nc.scalar.copy(bias_cols[:], bank[:, 0:O_TILES])

        def quant_attn(q):
            nc.vector.quantize_mx(out=attn_codes[q][:].bitcast(FP8X4), scales=attn_scales[q][:], in_=attn_kp[q][:].rearrange("p g n t -> p (g n t)"))

        def quant_hx(g):
            nc.vector.quantize_mx(out=hx_codes[g][:].bitcast(FP8X4), scales=hx_scales[g][:], in_=hx_kp[g][:].rearrange("p c t -> p (c t)"))

        def z_quarter(q):
            for part in range(QN // P):
                bank = bank_tile()
                for t in range(PACK):
                    for g in range(GROUPS):
                        cols = slice(QN * g + P * part, QN * g + P * (part + 1))
                        nc.tensor.matmul_mx(
                            out=bank[:, P * t : P * (t + 1)],
                            lhsT=hx_codes[g][:, P * t : P * (t + 1)].bitcast(FP8X4),
                            lhsT_scale=hx_scales[g][:, P * t : P * (t + 1)],
                            rhs=attn_codes[q][:, cols].bitcast(FP8X4),
                            rhs_scale=attn_scales[q][:, cols],
                            start=(g == 0),
                            stop=(g == GROUPS - 1),
                        )
                nc.scalar.copy(z_kp[q // 2][:, QN * (q % 2) + P * part : QN * (q % 2) + P * (part + 1), :], bank[:].rearrange("p (t n) -> p n t", t=PACK))

        def quant_z(h, cols):
            nc.vector.quantize_mx(out=z_codes[h][:, cols].bitcast(FP8X4), scales=z_scales[h][:, cols], in_=z_kp[h][:, cols, :].rearrange("p n t -> p (n t)"))

        y_banks = {}

        def y_matmul(a, h):
            y_banks[a, h] = bank_tile()
            nc.tensor.matmul_mx(
                out=y_banks[a, h][:],
                lhsT=words[:, 2 * P * a : 2 * P * (a + 1)].bitcast(FP4X4),
                lhsT_scale=word_scales[:, P * a : P * (a + 1)],
                rhs=z_codes[h][:].bitcast(FP8X4),
                rhs_scale=z_scales[h][:],
                start=True,
                stop=True,
            )

        def y_quarter(a, q):
            if q == 0:
                y_banks[a, 0] = bank_tile()
            cols = slice(QN * q, QN * (q + 1))
            nc.tensor.matmul_mx(
                out=y_banks[a, 0][:, cols],
                lhsT=words[:, 2 * P * a : 2 * P * (a + 1)].bitcast(FP4X4),
                lhsT_scale=word_scales[:, P * a : P * (a + 1)],
                rhs=z_codes[0][:, cols].bitcast(FP8X4),
                rhs_scale=z_scales[0][:, cols],
                start=True,
                stop=True,
            )

        def residual(a, h):
            return xs[a // X_TILES][:, a % X_TILES, HN * h : HN * (h + 1)]

        def finish_y(a, h):
            nc.vector.scalar_tensor_tensor(
                out=results[h][:, a, :], in0=y_banks[a, h][:], scalar=bias_cols[:, a : a + 1], in1=residual(a, h), op0=ADD, op1=ADD
            )

        partials = {}

        def shared_bias(a, h):
            partials[a, h] = temp.tile([P, HN], F32, name="partial", tag=f"partial{h * (1 - a // 4 % 2)}", align_bytes=256)
            nc.scalar.activation(partials[a, h][:], y_banks[a, h][:], ACT.Identity, bias=bias_cols[:, a : a + 1])
            nc.gpsimd.tensor_tensor(out=results[h][:, a, :], in0=partials[a, h][:], in1=residual(a, h), op=ADD)

        out_view = out.rearrange("b (a p) h w -> p a (b h w)", p=P)

        def store(h, first, count):
            nc.sync.dma_start(out=out_view[:, first : first + count, HN * h : HN * (h + 1)], in_=results[h][:, first : first + count, :])

        def y_round(r, h):
            y_matmul(4 * r + 3, h)
            shared_bias(4 * r + 3, h)
            for a in range(4 * r, 4 * r + 3):
                y_matmul(a, h)

        def finish_round(r, h, sizes):
            first = 4 * r
            for size in sizes:
                for a in range(first, min(first + size, 4 * r + 3)):
                    finish_y(a, h)
                store(h, first, size)
                first = first + size

        warm(3)
        spread(0, (0,))
        spread(0, (1,))
        spread(1, (0, 1))
        warm(2)
        fill_scale_row()
        first_product(0, (0,))
        first_product(0, (1,))
        first_product(1, (0, 1))
        product(1, 0)
        product(1, 1)
        for i in range(2):
            for g in range(GROUPS):
                hx_turn(i, g)
        attn_turn(0, 0)
        attn_turn(0, 1)
        attn_turn(1, 0)
        bias_turn()
        attn_turn(1, 1)
        busy(2)
        quant_hx(0)
        quant_hx(1)
        quant_attn(0)
        product(2, 0)
        quant_attn(1)
        z_quarter(0)
        z_quarter(1)
        product(2, 1)
        quant_z(0, slice(0, QN))
        product(3, 0)
        quant_z(0, slice(QN, HN))
        product(3, 1)
        attn_turn(2, 0)
        attn_turn(2, 1)
        for q in range(2):
            for a in (3, 0, 1, 2):
                y_quarter(a, q)
        shared_bias(3, 0)
        attn_turn(3, 0)
        attn_turn(3, 1)
        finish_round(0, 0, (1, 1, 2))
        y_round(1, 0)
        quant_attn(2)
        z_quarter(2)
        finish_round(1, 0, (1, 1, 2))
        y_round(2, 0)
        quant_attn(3)
        y_matmul(12, 0)
        z_quarter(3)
        finish_round(2, 0, (1, 1, 2))
        y_matmul(15, 0)
        shared_bias(15, 0)
        y_matmul(13, 0)
        y_matmul(14, 0)
        finish_y(12, 0)
        store(0, 12, 1)
        quant_z(1, slice(0, HN))
        finish_y(13, 0)
        store(0, 13, 1)
        finish_y(14, 0)
        store(0, 14, 2)
        y_round(0, 1)
        for r, sizes in enumerate(((2, 2), (4,), (4,), (4,))):
            if r + 1 < O_TILES // ROUND:
                y_round(r + 1, 1)
            finish_round(r, 1, sizes)
